import numpy as np
import ml_dtypes


def mxq(x, axis, fmt="e4m3"):
    dtype, down = {"e4m3": (ml_dtypes.float8_e4m3fn, 7), "e5m2": (ml_dtypes.float8_e5m2, 14)}[fmt]
    v = np.moveaxis(np.asarray(x, np.float32).astype(ml_dtypes.bfloat16).astype(np.float64), axis, -1)
    blocks = v.reshape(v.shape[:-1] + (-1, 32))
    amax = np.abs(blocks).max(-1, keepdims=True)
    byte = np.maximum(np.where(amax > 0, np.frexp(amax)[1] - 1 + 127, 0) - down, 1)
    scale = np.exp2(byte - 127.0)
    codes = (blocks / scale).astype(np.float32).astype(dtype).astype(np.float64)
    return np.moveaxis((codes * scale).reshape(v.shape), -1, axis)


WIDE = False


def mx_kscale(k):
    if not WIDE:
        return np.ones(k)
    levels = np.array([10, -10, 5, -5, 0])
    a = np.random.permutation(np.resize(levels, k // 512 * 4)).reshape(k // 512, 4)
    idx = np.arange(k)
    return np.exp2(a[idx // 512, idx % 128 // 32])


BF16 = ml_dtypes.bfloat16


def bf(x):
    return np.asarray(x, np.float32).astype(BF16)


def f64(x):
    return np.asarray(x).astype(np.float64)


E2M1 = np.array([0.0, 0.5, 1.0, 1.5, 2.0, 3.0, 4.0, 6.0, -0.0, -0.5, -1.0, -1.5, -2.0, -3.0, -4.0, -6.0])


def pack_weight(w, fmt):
    k, n = w.shape
    w = f64(bf(w)).reshape(k // 32, 32, n)
    amax = np.abs(w).max(1)
    if fmt == "e4m3":
        byte = np.frexp(amax)[1] - 1 + 127 - 7
    else:
        mant, ex = np.frexp(amax / 6.0)
        byte = np.where(mant > 0.5, ex, ex - 1) + 127
    byte = np.clip(np.where(amax > 0, byte, 1), 1, 254)
    scaled = (w * np.exp2(127.0 - byte)[:, None, :]).reshape(k, n).astype(np.float32)
    by_word = np.ascontiguousarray(scaled.reshape(k // 512, 128, 4, n).transpose(0, 1, 3, 2))
    if fmt == "e4m3":
        words = by_word.astype(ml_dtypes.float8_e4m3fn).view(np.uint8)
    else:
        c = by_word.astype(ml_dtypes.float4_e2m1fn).view(np.uint8) & 0xF
        words = c[..., 0::2] | (c[..., 1::2] << 4)
    return np.ascontiguousarray(words), np.ascontiguousarray(byte.astype(np.uint8).reshape(k // 512, 16, n))


def unpack_weight(words, scales, fmt):
    g, p, n, _ = words.shape
    if fmt == "e4m3":
        vals = np.ascontiguousarray(words).view(ml_dtypes.float8_e4m3fn).astype(np.float64)
    else:
        nib = np.empty((g, p, n, 4), np.uint8)
        nib[..., 0::2] = words & 0xF
        nib[..., 1::2] = words >> 4
        vals = E2M1[nib]
    vals = vals * np.repeat(np.exp2(scales.astype(np.float64) - 127.0), 8, axis=1)[..., None]
    return vals.transpose(0, 1, 3, 2).reshape(g * 512, n)


T, D, E, BLK = 512, 16384, 128, 512
EPS = 1e-05
FMT = "e4m3"


def setup_inputs():
    s = mx_kscale(D)
    rs = 10.0 ** np.random.uniform(-2.5, 0.5, (T, 1))
    h = bf((np.random.standard_normal((T, D)) + 0.3) * rs)
    ln_w = bf(np.random.standard_normal(D) * s)
    ln_b = bf(np.random.standard_normal(D) * 0.3 * s)
    w_q_words, w_q_scales = pack_weight(np.ascontiguousarray((np.random.standard_normal((E, D)) * 1.6 / np.sqrt(D) / s).T), FMT)
    w_k_words, w_k_scales = pack_weight(np.ascontiguousarray((np.random.standard_normal((E, D)) * 1.6 / np.sqrt(D) / s).T), FMT)
    w_v_words, w_v_scales = pack_weight(np.ascontiguousarray((np.random.standard_normal((E, D)) * 1.0 / np.sqrt(D) / s).T), FMT)
    return {"h": h,
            "ln_w": ln_w,
            "ln_b": ln_b,
            "w_q_words": w_q_words, "w_q_scales": w_q_scales,
            "w_k_words": w_k_words, "w_k_scales": w_k_scales,
            "w_v_words": w_v_words, "w_v_scales": w_v_scales}


def reference(h, ln_w, ln_b, w_q_words, w_q_scales, w_k_words, w_k_scales, w_v_words, w_v_scales):
    h = f64(h)
    mu = h.mean(-1, keepdims=True)
    var = np.square(h - mu).mean(-1, keepdims=True)
    h_norm = (h - mu) / np.sqrt(var + EPS) * f64(ln_w) + f64(ln_b)
    hq = mxq(h_norm, 1, "e4m3")
    q = hq @ unpack_weight(w_q_words, w_q_scales, FMT)
    k = hq @ unpack_weight(w_k_words, w_k_scales, FMT)
    v = hq @ unpack_weight(w_v_words, w_v_scales, FMT)
    return q, k, v

@@ -1,0 +1,205 @@
+from contextlib import ExitStack
+
+import concourse.mybir as mybir
+from concourse.masks import make_identity
+
+F32 = mybir.dt.float32
+BF16 = mybir.dt.bfloat16
+I32 = mybir.dt.int32
+U32 = mybir.dt.uint32
+U8 = mybir.dt.uint8
+FP8X4 = mybir.dt.float8_e4m3fn_x4
+ALU = mybir.AluOpType
+ACT = mybir.ActivationFunctionType
+
+P = 128
+PACK = 4
+K_PASS = P * PACK
+ROWS = 512
+D = 16384
+E = 128
+ROW_TILES = ROWS // P
+GROUPS = D // K_PASS
+EPS = 1e-5
+LOAD_COLS = 4096
+WORD_GROUPS = 8
+VECTOR_ROWS = 384
+RUN = 4
+BN_COLS = 512
+SCALAR_COLS = 2560
+VECTOR_CHUNKS = (D - 2 * SCALAR_COLS) // BN_COLS
+SLOT = 8
+
+FLOPS = 2 * ROWS * D * 3 * E
+
+
+def tile_toyattnsublayer_pa_k_kernel(
+    tc, h, ln_w, ln_b, w_q_words, w_q_scales, w_k_words, w_k_scales, w_v_words, w_v_scales, out_0, out_1, out_2
+):
+    nc = tc.nc
+    words_in = [w_q_words, w_k_words, w_v_words]
+    scales_in = [w_q_scales, w_k_scales, w_v_scales]
+    outs = [out_0, out_1, out_2]
+
+    with ExitStack() as ctx:
+        const = ctx.enter_context(tc.tile_pool(name="const", bufs=1))
+        small = ctx.enter_context(tc.tile_pool(name="small", bufs=1))
+        psum_acc = ctx.enter_context(tc.psum_pool(name="psum_acc", bufs=1))
+        psum_t = ctx.enter_context(tc.psum_pool(name="psum_t", bufs=5))
+
+        ident_f32 = const.tile([P, P], F32)
+        make_identity(nc, ident_f32[:])
+        ident_bf16 = const.tile([P, P], BF16)
+        make_identity(nc, ident_bf16[:])
+
+        w_planes = const.tile([P, 3, GROUPS, E], U8, align_bytes=64)
+        nc.vector.memset(w_planes[:].bitcast(I32), 0)
+        ln_rows = const.tile([P, K_PASS], BF16)
+        nc.vector.memset(ln_rows[:], 0.0)
+        w_words = const.tile([P, 3, GROUPS, E], U32, align_bytes=64)
+
+        h_sb = [const.tile([P, D], BF16, name="h_sb%d" % j) for j in range(ROW_TILES)]
+
+        def load_h(j):
+            for c in range(0, D, LOAD_COLS):
+                nc.sync.dma_start(out=h_sb[j][:, c : c + LOAD_COLS], in_=h[j * P : (j + 1) * P, c : c + LOAD_COLS])
+
+        load_h(0)
+        nc.sync.dma_start(out=ln_rows[0:GROUPS, :], in_=ln_w.rearrange("(g c) -> g c", c=K_PASS))
+        nc.sync.dma_start(out=ln_rows[GROUPS : 2 * GROUPS, :], in_=ln_b.rearrange("(g c) -> g c", c=K_PASS))
+        load_h(1)
+        for w in range(3):
+            for quad in range(4):
+                nc.sync.dma_start(
+                    out=w_planes[32 * quad : 32 * quad + 4, w, :, :].bitcast(I32),
+                    in_=scales_in[w][:, 4 * quad : 4 * quad + 4, :].rearrange("g q n -> q g n").bitcast(I32),
+                )
+        load_h(2)
+        load_h(3)
+        for g0 in range(0, GROUPS, WORD_GROUPS):
+            for w in range(3):
+                nc.sync.dma_start(
+                    out=w_words[:, w, g0 : g0 + WORD_GROUPS, :].bitcast(I32),
+                    in_=words_in[w].rearrange("g p n t -> p g (n t)")[:, g0 : g0 + WORD_GROUPS, :].bitcast(I32),
+                )
+
+        ln_t = psum_t.tile([P, PACK, P], BF16, tag="xt")
+        for t in range(PACK):
+            nc.tensor.transpose(ln_t[:, t, :], ln_rows[:, t:K_PASS:PACK], ident_bf16[:])
+        ln_cols = const.tile([P, PACK, 2 * GROUPS], F32)
+        nc.vector.tensor_copy(out=ln_cols[:], in_=ln_t[:, :, 0 : 2 * GROUPS])
+
+        warm = small.tile([P, 1], F32)
+        nc.vector.memset(warm[:], 1.0)
+        nc.scalar.sqrt(out=warm[:], in_=warm[:])
+        mean = []
+        rstd = []
+        with tc.tile_pool(name="scratch", bufs=2) as scratch:
+            for j in range(ROW_TILES):
+                stats = small.tile([P, VECTOR_CHUNKS + 1, SLOT], F32, name="stats%d" % j)
+                nc.vector.memset(stats[:, VECTOR_CHUNKS, 0:6], float(SCALAR_COLS))
+                ranges = [slice(0, SCALAR_COLS), slice(D - SCALAR_COLS, D)]
+                for a in range(2):
+                    total = small.tile([P, 1], F32, name="total%d_%d" % (j, a))
+                    unread = scratch.tile([P, SCALAR_COLS], BF16, name="unread", tag="unread")
+                    nc.scalar.activation(out=unread[:], in_=h_sb[j][:, ranges[a]], func=ACT.Identity, accum_out=total[:])
+                    nc.scalar.mul(out=stats[:, VECTOR_CHUNKS, 3 * a + 1 : 3 * a + 2], in_=total[:], mul=1.0 / SCALAR_COLS)
+                    unread = scratch.tile([P, SCALAR_COLS], BF16, name="unread", tag="unread")
+                    nc.scalar.activation(
+                        out=unread[:],
+                        in_=h_sb[j][:, ranges[a]],
+                        func=ACT.Square,
+                        scale=-1.0,
+                        bias=stats[:, VECTOR_CHUNKS, 3 * a + 1 : 3 * a + 2],
+                        accum_out=stats[:, VECTOR_CHUNKS, 3 * a + 2 : 3 * a + 3],
+                    )
+                for c in range(VECTOR_CHUNKS):
+                    first = SCALAR_COLS + c * BN_COLS
+                    nc.vector.bn_stats(out=stats[:, c, 0:6], in_=h_sb[j][:, first : first + BN_COLS])
+                mean_var = small.tile([P, 2], F32, name="mean_var%d" % j)
+                nc.vector.bn_aggr(out=mean_var[:], in_=stats[:, :, 0:6])
+                var_eps = small.tile([P, 1], F32, name="var_eps%d" % j)
+                nc.vector.tensor_scalar_add(out=var_eps[:], in0=mean_var[:, 1:2], scalar1=EPS)
+                std = small.tile([P, 1], F32, name="std%d" % j)
+                nc.scalar.sqrt(out=std[:], in_=var_eps[:])
+                rstd_j = small.tile([P, 1], F32, name="rstd%d" % j)
+                nc.vector.reciprocal(out=rstd_j[:], in_=std[:])
+                mean.append(mean_var[:, 0:1])
+                rstd.append(rstd_j[:, 0:1])
+
+        work = ctx.enter_context(tc.tile_pool(name="work", bufs=8))
+        stage = ctx.enter_context(tc.tile_pool(name="stage", bufs=2))
+
+        acc = [psum_acc.tile([P, ROWS], F32, name="acc%d" % w) for w in range(3)]
+        for g in range(GROUPS):
+            cols = slice(g * K_PASS, (g + 1) * K_PASS)
+            unit = []
+            for j in range(ROW_TILES):
+                unit_j = work.tile([P, PACK, P], F32, name="unit_j", tag="work")
+                nc.vector.tensor_scalar(
+                    out=unit_j[:],
+                    in0=h_sb[j][:, cols].rearrange("r (p t) -> r t p", t=PACK),
+                    scalar1=mean[j],
+                    scalar2=rstd[j],
+                    op0=ALU.subtract,
+                    op1=ALU.mult,
+                )
+                unit.append(unit_j)
+            planes = stage.tile([P, PACK, ROWS], BF16)
+            for t in range(PACK):
+                xt = psum_t.tile([P, ROWS], F32, tag="xt")
+                for j in range(ROW_TILES):
+                    nc.tensor.transpose(xt[:, j * P : (j + 1) * P], unit[j][:, t, :], ident_f32[:])
+                nc.scalar.activation(
+                    out=planes[:, t, :],
+                    in_=xt[:],
+                    func=ACT.Identity,
+                    scale=ln_cols[:, t, g : g + 1],
+                    bias=ln_cols[:, t, GROUPS + g : GROUPS + g + 1],
+                )
+            grouped = stage.tile([P, ROWS, PACK], BF16, align_bytes=64)
+            nc.vector.tensor_copy(
+                out=grouped[:, 0:VECTOR_ROWS, :].rearrange("p (c i) t -> p c t i", i=RUN),
+                in_=planes[:, :, 0:VECTOR_ROWS].rearrange("p t (c i) -> p c t i", i=RUN),
+            )
+            nc.scalar.copy(
+                out=grouped[:, VECTOR_ROWS:ROWS, :].rearrange("p (c i) t -> p c t i", i=RUN),
+                in_=planes[:, :, VECTOR_ROWS:ROWS].rearrange("p t (c i) -> p c t i", i=RUN),
+            )
+            codes = stage.tile([P, ROWS], U32, align_bytes=64)
+            code_scales = stage.tile([P, ROWS], U8, align_bytes=64)
+            nc.vector.quantize_mx(
+                out=codes[:].bitcast(FP8X4),
+                scales=code_scales[:],
+                in_=grouped[:].rearrange("p r t -> p (r t)"),
+            )
+            for w in range(3):
+                nc.tensor.matmul_mx(
+                    out=acc[w][:],
+                    lhsT=w_words[:, w, g, :].bitcast(FP8X4),
+                    lhsT_scale=w_planes[:, w, g, :],
+                    rhs=codes[:].bitcast(FP8X4),
+                    rhs_scale=code_scales[:],
+                    start=(g == 0),
+                    stop=(g == GROUPS - 1),
+                )
+
+        by_feature = []
+        for w in range(3):
+            by_feature_w = work.tile([P, ROWS], F32, name="by_feature_w", tag="work")
+            if w == 1:
+                nc.scalar.copy(out=by_feature_w[:], in_=acc[w][:])
+            else:
+                nc.vector.tensor_copy(out=by_feature_w[:], in_=acc[w][:])
+            by_feature.append(by_feature_w)
+        for j in range(ROW_TILES):
+            turned = psum_t.tile([P, 3, E], F32, tag="xt")
+            for w in range(3):
+                nc.tensor.transpose(turned[:, w, :], by_feature[w][:, j * P : (j + 1) * P], ident_f32[:])
+            by_row = work.tile([P, 3, E], F32, name="by_row", tag="work")
+            if j % 2 == 0:
+                nc.vector.tensor_copy(out=by_row[:], in_=turned[:])
+            else:
+                nc.scalar.copy(out=by_row[:], in_=turned[:])
+            for w in range(3):
+                nc.sync.dma_start(out=outs[w][j * P : (j + 1) * P, :], in_=by_row[:, w, :])

@@ -131,58 +131,83 @@ def tile_toyattnsublayer_pa_k_kernel(
         stage = ctx.enter_context(tc.tile_pool(name="stage", bufs=2))
 
         acc = [psum_acc.tile([P, ROWS], F32, name="acc%d" % w) for w in range(3)]
-        for g in range(GROUPS):
+        unit = {}
+        planes = {}
+        grouped = {}
+        codes = {}
+        code_scales = {}
+
+        def normalise(g):
             cols = slice(g * K_PASS, (g + 1) * K_PASS)
-            unit = []
             for j in range(ROW_TILES):
-                unit_j = work.tile([P, PACK, P], F32, name="unit_j", tag="work")
+                unit[g, j] = work.tile([P, PACK, P], F32, name="unit", tag="work")
                 nc.vector.tensor_scalar(
-                    out=unit_j[:],
+                    out=unit[g, j][:],
                     in0=h_sb[j][:, cols].rearrange("r (p t) -> r t p", t=PACK),
                     scalar1=mean[j],
                     scalar2=rstd[j],
                     op0=ALU.subtract,
                     op1=ALU.mult,
                 )
-                unit.append(unit_j)
-            planes = stage.tile([P, PACK, ROWS], BF16)
+
+        def turn_and_scale(g):
+            planes[g] = stage.tile([P, PACK, ROWS], BF16, name="planes", tag="planes")
             for t in range(PACK):
                 xt = psum_t.tile([P, ROWS], F32, tag="xt")
                 for j in range(ROW_TILES):
-                    nc.tensor.transpose(xt[:, j * P : (j + 1) * P], unit[j][:, t, :], ident_f32[:])
+                    nc.tensor.transpose(xt[:, j * P : (j + 1) * P], unit[g, j][:, t, :], ident_f32[:])
                 nc.scalar.activation(
-                    out=planes[:, t, :],
+                    out=planes[g][:, t, :],
                     in_=xt[:],
                     func=ACT.Identity,
                     scale=ln_cols[:, t, g : g + 1],
                     bias=ln_cols[:, t, GROUPS + g : GROUPS + g + 1],
                 )
-            grouped = stage.tile([P, ROWS, PACK], BF16, align_bytes=64)
+
+        def regroup(g):
+            grouped[g] = stage.tile([P, ROWS, PACK], BF16, name="grouped", tag="grouped", align_bytes=64)
             nc.vector.tensor_copy(
-                out=grouped[:, 0:VECTOR_ROWS, :].rearrange("p (c i) t -> p c t i", i=RUN),
-                in_=planes[:, :, 0:VECTOR_ROWS].rearrange("p t (c i) -> p c t i", i=RUN),
+                out=grouped[g][:, 0:VECTOR_ROWS, :].rearrange("p (c i) t -> p c t i", i=RUN),
+                in_=planes[g][:, :, 0:VECTOR_ROWS].rearrange("p t (c i) -> p c t i", i=RUN),
             )
             nc.scalar.copy(
-                out=grouped[:, VECTOR_ROWS:ROWS, :].rearrange("p (c i) t -> p c t i", i=RUN),
-                in_=planes[:, :, VECTOR_ROWS:ROWS].rearrange("p t (c i) -> p c t i", i=RUN),
+                out=grouped[g][:, VECTOR_ROWS:ROWS, :].rearrange("p (c i) t -> p c t i", i=RUN),
+                in_=planes[g][:, :, VECTOR_ROWS:ROWS].rearrange("p t (c i) -> p c t i", i=RUN),
             )
-            codes = stage.tile([P, ROWS], U32, align_bytes=64)
-            code_scales = stage.tile([P, ROWS], U8, align_bytes=64)
+
+        def quantise(g):
+            codes[g] = stage.tile([P, ROWS], U32, name="codes", tag="codes", align_bytes=64)
+            code_scales[g] = stage.tile([P, ROWS], U8, name="code_scales", tag="code_scales", align_bytes=64)
             nc.vector.quantize_mx(
-                out=codes[:].bitcast(FP8X4),
-                scales=code_scales[:],
-                in_=grouped[:].rearrange("p r t -> p (r t)"),
+                out=codes[g][:].bitcast(FP8X4),
+                scales=code_scales[g][:],
+                in_=grouped[g][:].rearrange("p r t -> p (r t)"),
             )
+
+        def project(g):
             for w in range(3):
                 nc.tensor.matmul_mx(
                     out=acc[w][:],
                     lhsT=w_words[:, w, g, :].bitcast(FP8X4),
                     lhsT_scale=w_planes[:, w, g, :],
-                    rhs=codes[:].bitcast(FP8X4),
-                    rhs_scale=code_scales[:],
+                    rhs=codes[g][:].bitcast(FP8X4),
+                    rhs_scale=code_scales[g][:],
                     start=(g == 0),
                     stop=(g == GROUPS - 1),
                 )
+
+        with tc.manual_schedule():
+            for step in range(GROUPS + 4):
+                if step < GROUPS:
+                    normalise(step)
+                if 0 <= step - 1 < GROUPS:
+                    turn_and_scale(step - 1)
+                if 0 <= step - 2 < GROUPS:
+                    regroup(step - 2)
+                if 0 <= step - 3 < GROUPS:
+                    quantise(step - 3)
+                if 0 <= step - 4 < GROUPS:
+                    project(step - 4)
 
         by_feature = []
         for w in range(3):

@@ -23,7 +23,7 @@ GROUPS = D // K_PASS
 EPS = 1e-5
 LOAD_COLS = 4096
 WORD_GROUPS = 8
-VECTOR_ROWS = 384
+VECTOR_ROWS = 512
 RUN = 4
 BN_COLS = 512
 SCALAR_COLS = 2560
@@ -170,10 +170,11 @@ def tile_toyattnsublayer_pa_k_kernel(
                 out=grouped[g][:, 0:VECTOR_ROWS, :].rearrange("p (c i) t -> p c t i", i=RUN),
                 in_=planes[g][:, :, 0:VECTOR_ROWS].rearrange("p t (c i) -> p c t i", i=RUN),
             )
-            nc.scalar.copy(
-                out=grouped[g][:, VECTOR_ROWS:ROWS, :].rearrange("p (c i) t -> p c t i", i=RUN),
-                in_=planes[g][:, :, VECTOR_ROWS:ROWS].rearrange("p t (c i) -> p c t i", i=RUN),
-            )
+            if VECTOR_ROWS < ROWS:
+                nc.scalar.copy(
+                    out=grouped[g][:, VECTOR_ROWS:ROWS, :].rearrange("p (c i) t -> p c t i", i=RUN),
+                    in_=planes[g][:, :, VECTOR_ROWS:ROWS].rearrange("p t (c i) -> p c t i", i=RUN),
+                )
 
         def quantise(g):
             codes[g] = stage.tile([P, ROWS], U32, name="codes", tag="codes", align_bytes=64)

@@ -22,13 +22,18 @@ ROW_TILES = ROWS // P
 GROUPS = D // K_PASS
 EPS = 1e-5
 LOAD_COLS = 4096
-WORD_GROUPS = 8
-VECTOR_ROWS = 512
+WORD_GROUPS = 4
 RUN = 4
 BN_COLS = 512
-SCALAR_COLS = 2560
+SCALAR_COLS = 3328
+SUM_BLOCKS = 19
+SUM_COLS = SUM_BLOCKS * P
 VECTOR_CHUNKS = (D - 2 * SCALAR_COLS) // BN_COLS
 SLOT = 8
+FINISH_AT = 4
+EARLY_COLS = 1024
+SPARE = 20
+UNITS = 2 * SPARE - 1
 
 FLOPS = 2 * ROWS * D * 3 * E
 
@@ -47,115 +52,230 @@ def tile_toyattnsublayer_pa_k_kernel(
         psum_acc = ctx.enter_context(tc.psum_pool(name="psum_acc", bufs=1))
         psum_t = ctx.enter_context(tc.psum_pool(name="psum_t", bufs=5))
 
-        ident_f32 = const.tile([P, P], F32)
-        make_identity(nc, ident_f32[:])
+        warm = small.tile([P, 1], F32)
+        nc.gpsimd.memset(warm[:], 1.0)
+        nc.scalar.sqrt(out=warm[:], in_=warm[:])
         ident_bf16 = const.tile([P, P], BF16)
         make_identity(nc, ident_bf16[:])
-
+        stats = []
+        for j in range(ROW_TILES):
+            stats_j = small.tile([P, VECTOR_CHUNKS + 1, SLOT], F32, name="stats%d" % j)
+            nc.gpsimd.memset(stats_j[:, VECTOR_CHUNKS, 0:6], float(SCALAR_COLS))
+            stats.append(stats_j)
+        ident_f32 = const.tile([P, P], F32)
+        make_identity(nc, ident_f32[:])
         w_planes = const.tile([P, 3, GROUPS, E], U8, align_bytes=64)
-        nc.vector.memset(w_planes[:].bitcast(I32), 0)
+        nc.gpsimd.memset(w_planes[:].bitcast(I32), 0)
         ln_rows = const.tile([P, K_PASS], BF16)
-        nc.vector.memset(ln_rows[:], 0.0)
-        w_words = const.tile([P, 3, GROUPS, E], U32, align_bytes=64)
+        nc.gpsimd.memset(ln_rows[:], 0.0)
+        spare = const.tile([P, SPARE, PACK, P], F32)
 
         h_sb = [const.tile([P, D], BF16, name="h_sb%d" % j) for j in range(ROW_TILES)]
 
-        def load_h(j):
-            for c in range(0, D, LOAD_COLS):
-                nc.sync.dma_start(out=h_sb[j][:, c : c + LOAD_COLS], in_=h[j * P : (j + 1) * P, c : c + LOAD_COLS])
+        def load_h(j, first, last):
+            nc.sync.dma_start(out=h_sb[j][:, first:last], in_=h[j * P : (j + 1) * P, first:last])
 
-        load_h(0)
+        load_h(0, SCALAR_COLS, SCALAR_COLS + EARLY_COLS)
+        load_h(0, SUM_COLS, SCALAR_COLS)
+        load_h(0, SCALAR_COLS + EARLY_COLS, SCALAR_COLS + 3 * EARLY_COLS)
+        load_h(0, 0, SUM_COLS)
+        load_h(0, SCALAR_COLS + 3 * EARLY_COLS, SCALAR_COLS + 5 * EARLY_COLS)
+        load_h(0, SCALAR_COLS + 5 * EARLY_COLS, D - SCALAR_COLS)
+        load_h(0, D - SCALAR_COLS, D)
+        for j in range(1, ROW_TILES):
+            for c in range(0, D, LOAD_COLS):
+                load_h(j, c, c + LOAD_COLS)
         nc.sync.dma_start(out=ln_rows[0:GROUPS, :], in_=ln_w.rearrange("(g c) -> g c", c=K_PASS))
         nc.sync.dma_start(out=ln_rows[GROUPS : 2 * GROUPS, :], in_=ln_b.rearrange("(g c) -> g c", c=K_PASS))
-        load_h(1)
         for w in range(3):
             for quad in range(4):
                 nc.sync.dma_start(
                     out=w_planes[32 * quad : 32 * quad + 4, w, :, :].bitcast(I32),
                     in_=scales_in[w][:, 4 * quad : 4 * quad + 4, :].rearrange("g q n -> q g n").bitcast(I32),
                 )
-        load_h(2)
-        load_h(3)
-        for g0 in range(0, GROUPS, WORD_GROUPS):
+        words_pool = ctx.enter_context(tc.tile_pool(name="words", bufs=2))
+        w_words = []
+
+        def load_words():
+            g0 = len(w_words) * WORD_GROUPS
+            chunk = words_pool.tile([P, 3, WORD_GROUPS, E], U32, name="chunk", tag="chunk", align_bytes=64)
+            w_words.append(chunk)
             for w in range(3):
                 nc.sync.dma_start(
-                    out=w_words[:, w, g0 : g0 + WORD_GROUPS, :].bitcast(I32),
+                    out=chunk[:, w, :, :].bitcast(I32),
                     in_=words_in[w].rearrange("g p n t -> p g (n t)")[:, g0 : g0 + WORD_GROUPS, :].bitcast(I32),
                 )
 
-        ln_t = psum_t.tile([P, PACK, P], BF16, tag="xt")
-        for t in range(PACK):
-            nc.tensor.transpose(ln_t[:, t, :], ln_rows[:, t:K_PASS:PACK], ident_bf16[:])
-        ln_cols = const.tile([P, PACK, 2 * GROUPS], F32)
-        nc.vector.tensor_copy(out=ln_cols[:], in_=ln_t[:, :, 0 : 2 * GROUPS])
+        load_words()
+        load_words()
 
-        warm = small.tile([P, 1], F32)
-        nc.vector.memset(warm[:], 1.0)
-        nc.scalar.sqrt(out=warm[:], in_=warm[:])
-        mean = []
-        rstd = []
-        with tc.tile_pool(name="scratch", bufs=2) as scratch:
-            for j in range(ROW_TILES):
-                stats = small.tile([P, VECTOR_CHUNKS + 1, SLOT], F32, name="stats%d" % j)
-                nc.vector.memset(stats[:, VECTOR_CHUNKS, 0:6], float(SCALAR_COLS))
-                ranges = [slice(0, SCALAR_COLS), slice(D - SCALAR_COLS, D)]
-                for a in range(2):
-                    total = small.tile([P, 1], F32, name="total%d_%d" % (j, a))
-                    unread = scratch.tile([P, SCALAR_COLS], BF16, name="unread", tag="unread")
-                    nc.scalar.activation(out=unread[:], in_=h_sb[j][:, ranges[a]], func=ACT.Identity, accum_out=total[:])
-                    nc.scalar.mul(out=stats[:, VECTOR_CHUNKS, 3 * a + 1 : 3 * a + 2], in_=total[:], mul=1.0 / SCALAR_COLS)
-                    unread = scratch.tile([P, SCALAR_COLS], BF16, name="unread", tag="unread")
-                    nc.scalar.activation(
-                        out=unread[:],
-                        in_=h_sb[j][:, ranges[a]],
-                        func=ACT.Square,
-                        scale=-1.0,
-                        bias=stats[:, VECTOR_CHUNKS, 3 * a + 1 : 3 * a + 2],
-                        accum_out=stats[:, VECTOR_CHUNKS, 3 * a + 2 : 3 * a + 3],
+        mean = {}
+        rstd = {}
+        var_eps = {}
+
+        def column(name):
+            return small.tile([P, 1], F32, name=name)
+
+        def vector_chunk(j, c):
+            first = SCALAR_COLS + c * BN_COLS
+            nc.vector.bn_stats(out=stats[j][:, c, 0:6], in_=h_sb[j][:, first : first + BN_COLS])
+
+        def sum_blocks(j):
+            sums = [psum_t.tile([P, P], F32, name="sums%d" % a, tag="xt") for a in range(2)]
+            for a in range(2):
+                first = a * (D - SCALAR_COLS)
+                for b in range(SUM_BLOCKS):
+                    nc.tensor.matmul(
+                        out=sums[a][:],
+                        lhsT=ident_bf16[:],
+                        rhs=h_sb[j][:, first + b * P : first + (b + 1) * P],
+                        start=(b == 0),
+                        stop=(b == SUM_BLOCKS - 1),
                     )
-                for c in range(VECTOR_CHUNKS):
-                    first = SCALAR_COLS + c * BN_COLS
-                    nc.vector.bn_stats(out=stats[:, c, 0:6], in_=h_sb[j][:, first : first + BN_COLS])
-                mean_var = small.tile([P, 2], F32, name="mean_var%d" % j)
-                nc.vector.bn_aggr(out=mean_var[:], in_=stats[:, :, 0:6])
-                var_eps = small.tile([P, 1], F32, name="var_eps%d" % j)
-                nc.vector.tensor_scalar_add(out=var_eps[:], in0=mean_var[:, 1:2], scalar1=EPS)
-                std = small.tile([P, 1], F32, name="std%d" % j)
-                nc.scalar.sqrt(out=std[:], in_=var_eps[:])
-                rstd_j = small.tile([P, 1], F32, name="rstd%d" % j)
-                nc.vector.reciprocal(out=rstd_j[:], in_=std[:])
-                mean.append(mean_var[:, 0:1])
-                rstd.append(rstd_j[:, 0:1])
+            return sums
 
-        work = ctx.enter_context(tc.tile_pool(name="work", bufs=8))
+        def scalar_sum(j, a, scratch):
+            first = a * (D - SCALAR_COLS)
+            own = column("own%d_%d" % (j, a))
+            unread = scratch.tile([P, SCALAR_COLS], BF16, name="unread", tag="unread")
+            nc.scalar.activation(
+                out=unread[:, 0 : SCALAR_COLS - SUM_COLS],
+                in_=h_sb[j][:, first + SUM_COLS : first + SCALAR_COLS],
+                func=ACT.Identity,
+                scale=1.0 / (SCALAR_COLS * P),
+                accum_out=own[:],
+            )
+            return own
+
+        def scalar_moments(j, a, own, sums, scratch):
+            first = a * (D - SCALAR_COLS)
+            shift = stats[j][:, 0, 1:2]
+            mean_at, m2_at = [stats[j][:, VECTOR_CHUNKS, 3 * a + i : 3 * a + i + 1] for i in (1, 2)]
+            squares = column("squares%d_%d" % (j, a))
+            unread = scratch.tile([P, SCALAR_COLS], BF16, name="unread", tag="unread")
+            nc.scalar.activation(
+                out=unread[:],
+                in_=h_sb[j][:, first : first + SCALAR_COLS],
+                func=ACT.Square,
+                scale=-1.0,
+                bias=shift,
+                accum_out=squares[:],
+            )
+            unread = scratch.tile([P, SCALAR_COLS], BF16, name="unread", tag="unread")
+            nc.scalar.activation(
+                out=unread[:, 0:P],
+                in_=sums[a][:],
+                func=ACT.Identity,
+                scale=1.0 / SCALAR_COLS,
+                bias=own[:],
+                accum_out=mean_at,
+            )
+            offset = column("offset%d_%d" % (j, a))
+            nc.scalar.activation(out=offset[:], in_=mean_at, func=ACT.Square, scale=-1.0, bias=shift)
+            nc.scalar.activation(out=m2_at, in_=offset[:], func=ACT.Identity, scale=-float(SCALAR_COLS), bias=squares[:])
+
+        def aggregate(j):
+            mean_var = small.tile([P, 2], F32, name="mean_var%d" % j)
+            nc.vector.bn_aggr(out=mean_var[:], in_=stats[j][:, :, 0:6])
+            var_eps[j] = column("var_eps%d" % j)
+            nc.vector.tensor_scalar_add(out=var_eps[j][:], in0=mean_var[:, 1:2], scalar1=EPS)
+            mean[j] = mean_var[:, 0:1]
+
+        def root(j):
+            nc.scalar.sqrt(out=var_eps[j][:], in_=var_eps[j][:])
+
+        def invert(j):
+            rstd_j = column("rstd%d" % j)
+            nc.vector.reciprocal(out=rstd_j[:], in_=var_eps[j][:])
+            rstd[j] = rstd_j[:, 0:1]
+
+        early = [(0, g) for g in range(GROUPS)] + [(1, g) for g in range(2 * GROUPS - UNITS, GROUPS)]
+        unit = {}
+
+        def unit_columns(j, g):
+            return h_sb[j][:, g * K_PASS : (g + 1) * K_PASS].rearrange("r (p t) -> r t p", t=PACK)
+
+        def normalise_early(j):
+            minus = column("minus%d" % j)
+            nc.gpsimd.tensor_scalar(
+                out=minus[:], in0=mean[j], scalar1=rstd[j], scalar2=-1.0, op0=ALU.mult, op1=ALU.mult
+            )
+            for n, (row_tile, g) in enumerate(early):
+                if row_tile == j:
+                    if n < SPARE:
+                        unit[j, g] = spare[:, n, :, :]
+                    else:
+                        used_j, used_g = early[2 * (n - SPARE)]
+                        used = h_sb[used_j][:, used_g * K_PASS : (used_g + 2) * K_PASS].bitcast(F32)
+                        unit[j, g] = used.rearrange("r (t p) -> r t p", t=PACK)
+                    nc.gpsimd.tensor_scalar(
+                        out=unit[j, g],
+                        in0=unit_columns(j, g),
+                        scalar1=rstd[j],
+                        scalar2=minus[:],
+                        op0=ALU.mult,
+                        op1=ALU.add,
+                    )
+
+        with tc.manual_schedule(), tc.tile_pool(name="scratch", bufs=2) as scratch:
+            for j in range(ROW_TILES):
+                sums = sum_blocks(j)
+                for c in range(FINISH_AT):
+                    vector_chunk(j, c)
+                own = scalar_sum(j, 0, scratch)
+                if j > 0:
+                    aggregate(j - 1)
+                    root(j - 1)
+                for c in range(FINISH_AT, 2 * FINISH_AT):
+                    vector_chunk(j, c)
+                if j > 0:
+                    invert(j - 1)
+                    if j <= 2:
+                        normalise_early(j - 1)
+                for c in range(2 * FINISH_AT, VECTOR_CHUNKS):
+                    vector_chunk(j, c)
+                scalar_moments(j, 0, own, sums, scratch)
+                own = scalar_sum(j, 1, scratch)
+                scalar_moments(j, 1, own, sums, scratch)
+            aggregate(ROW_TILES - 1)
+            root(ROW_TILES - 1)
+
+            ln_t = psum_t.tile([P, PACK, P], BF16, tag="xt")
+            for t in range(PACK):
+                nc.tensor.transpose(ln_t[:, t, :], ln_rows[:, t:K_PASS:PACK], ident_bf16[:])
+            ln_cols = const.tile([P, PACK, 2 * GROUPS], F32)
+            nc.vector.tensor_copy(out=ln_cols[:], in_=ln_t[:, :, 0 : 2 * GROUPS])
+            invert(ROW_TILES - 1)
+
+        work = ctx.enter_context(tc.tile_pool(name="work", bufs=6))
         stage = ctx.enter_context(tc.tile_pool(name="stage", bufs=2))
 
         acc = [psum_acc.tile([P, ROWS], F32, name="acc%d" % w) for w in range(3)]
-        unit = {}
         planes = {}
         grouped = {}
         codes = {}
         code_scales = {}
 
-        def normalise(g):
-            cols = slice(g * K_PASS, (g + 1) * K_PASS)
+        def normalise_rest(g):
             for j in range(ROW_TILES):
-                unit[g, j] = work.tile([P, PACK, P], F32, name="unit", tag="work")
-                nc.vector.tensor_scalar(
-                    out=unit[g, j][:],
-                    in0=h_sb[j][:, cols].rearrange("r (p t) -> r t p", t=PACK),
-                    scalar1=mean[j],
-                    scalar2=rstd[j],
-                    op0=ALU.subtract,
-                    op1=ALU.mult,
-                )
+                if (j, g) not in unit:
+                    made = work.tile([P, PACK, P], F32, name="made", tag="work")
+                    unit[j, g] = made[:]
+                    nc.vector.tensor_scalar(
+                        out=unit[j, g],
+                        in0=unit_columns(j, g),
+                        scalar1=mean[j],
+                        scalar2=rstd[j],
+                        op0=ALU.subtract,
+                        op1=ALU.mult,
+                    )
 
         def turn_and_scale(g):
             planes[g] = stage.tile([P, PACK, ROWS], BF16, name="planes", tag="planes")
             for t in range(PACK):
                 xt = psum_t.tile([P, ROWS], F32, tag="xt")
                 for j in range(ROW_TILES):
-                    nc.tensor.transpose(xt[:, j * P : (j + 1) * P], unit[g, j][:, t, :], ident_f32[:])
+                    nc.tensor.transpose(xt[:, j * P : (j + 1) * P], unit[j, g][:, t, :], ident_f32[:])
                 nc.scalar.activation(
                     out=planes[g][:, t, :],
                     in_=xt[:],
@@ -167,14 +287,9 @@ def tile_toyattnsublayer_pa_k_kernel(
         def regroup(g):
             grouped[g] = stage.tile([P, ROWS, PACK], BF16, name="grouped", tag="grouped", align_bytes=64)
             nc.vector.tensor_copy(
-                out=grouped[g][:, 0:VECTOR_ROWS, :].rearrange("p (c i) t -> p c t i", i=RUN),
-                in_=planes[g][:, :, 0:VECTOR_ROWS].rearrange("p t (c i) -> p c t i", i=RUN),
+                out=grouped[g][:].rearrange("p (c i) t -> p c t i", i=RUN),
+                in_=planes[g][:].rearrange("p t (c i) -> p c t i", i=RUN),
             )
-            if VECTOR_ROWS < ROWS:
-                nc.scalar.copy(
-                    out=grouped[g][:, VECTOR_ROWS:ROWS, :].rearrange("p (c i) t -> p c t i", i=RUN),
-                    in_=planes[g][:, :, VECTOR_ROWS:ROWS].rearrange("p t (c i) -> p c t i", i=RUN),
-                )
 
         def quantise(g):
             codes[g] = stage.tile([P, ROWS], U32, name="codes", tag="codes", align_bytes=64)
@@ -189,7 +304,7 @@ def tile_toyattnsublayer_pa_k_kernel(
             for w in range(3):
                 nc.tensor.matmul_mx(
                     out=acc[w][:],
-                    lhsT=w_words[:, w, g, :].bitcast(FP8X4),
+                    lhsT=w_words[g // WORD_GROUPS][:, w, g % WORD_GROUPS, :].bitcast(FP8X4),
                     lhsT_scale=w_planes[:, w, g, :],
                     rhs=codes[g][:].bitcast(FP8X4),
                     rhs_scale=code_scales[g][:],
@@ -200,7 +315,7 @@ def tile_toyattnsublayer_pa_k_kernel(
         with tc.manual_schedule():
             for step in range(GROUPS + 4):
                 if step < GROUPS:
-                    normalise(step)
+                    normalise_rest(step)
                 if 0 <= step - 1 < GROUPS:
                     turn_and_scale(step - 1)
                 if 0 <= step - 2 < GROUPS:
@@ -209,6 +324,8 @@ def tile_toyattnsublayer_pa_k_kernel(
                     quantise(step - 3)
                 if 0 <= step - 4 < GROUPS:
                     project(step - 4)
+                    if (step - 3) % WORD_GROUPS == 0 and len(w_words) * WORD_GROUPS < GROUPS:
+                        load_words()
 
         by_feature = []
         for w in range(3):

@@ -32,7 +32,7 @@ VECTOR_CHUNKS = (D - 2 * SCALAR_COLS) // BN_COLS
 SLOT = 8
 FINISH_AT = 4
 EARLY_COLS = 1024
-SPARE = 20
+SPARE = 22
 UNITS = 2 * SPARE - 1
 
 FLOPS = 2 * ROWS * D * 3 * E
@@ -121,7 +121,7 @@ def tile_toyattnsublayer_pa_k_kernel(
             nc.vector.bn_stats(out=stats[j][:, c, 0:6], in_=h_sb[j][:, first : first + BN_COLS])
 
         def sum_blocks(j):
-            sums = [psum_t.tile([P, P], F32, name="sums%d" % a, tag="xt") for a in range(2)]
+            sums = [psum_acc.tile([P, P], F32, name="sums%d" % a, tag="acc%d" % ((2 * j + a) % 3)) for a in range(2)]
             for a in range(2):
                 first = a * (D - SCALAR_COLS)
                 for b in range(SUM_BLOCKS):
@@ -217,132 +217,200 @@ def tile_toyattnsublayer_pa_k_kernel(
                         op1=ALU.add,
                     )
 
+        work = ctx.enter_context(tc.tile_pool(name="work", bufs=6))
+
+        def normalise_one(j, g):
+            made = work.tile([P, PACK, P], F32, name="made", tag="work")
+            unit[j, g] = made[:]
+            nc.vector.tensor_scalar(
+                out=unit[j, g],
+                in0=unit_columns(j, g),
+                scalar1=mean[j],
+                scalar2=rstd[j],
+                op0=ALU.subtract,
+                op1=ALU.mult,
+            )
+
+        turned_units = {}
+
+        def turn(g, tiles):
+            if g not in turned_units:
+                turned_units[g] = [psum_t.tile([P, ROWS], F32, name="xt%d" % t, tag="xt") for t in range(PACK)]
+            for t in range(PACK):
+                for j in tiles:
+                    nc.tensor.transpose(
+                        turned_units[g][t][:, j * P : (j + 1) * P], unit[j, g][:, t, :], ident_f32[:]
+                    )
+
+        def keep_busy(passes, columns):
+            unread = psum_t.tile([P, ROWS], F32, name="unread_product", tag="xt")
+            for i in range(passes):
+                nc.tensor.matmul_mx(
+                    out=unread[:, 0:columns],
+                    lhsT=w_words[0][:, 0, 0, :].bitcast(FP8X4),
+                    lhsT_scale=w_planes[:, 0, 0, :],
+                    rhs=w_words[0][:, 0, :, :].rearrange("p g n -> p (g n)")[:, 0:columns].bitcast(FP8X4),
+                    rhs_scale=w_planes[:, 0, 0:WORD_GROUPS, :].rearrange("p g n -> p (g n)")[:, 0:columns],
+                    start=True,
+                    stop=True,
+                )
+
         with tc.manual_schedule(), tc.tile_pool(name="scratch", bufs=2) as scratch:
             for j in range(ROW_TILES):
                 sums = sum_blocks(j)
                 for c in range(FINISH_AT):
                     vector_chunk(j, c)
-                own = scalar_sum(j, 0, scratch)
                 if j > 0:
                     aggregate(j - 1)
+                if j == 1:
                     root(j - 1)
-                for c in range(FINISH_AT, 2 * FINISH_AT):
+                own = scalar_sum(j, 0, scratch)
+                if j > 1:
+                    root(j - 1)
+                finish = FINISH_AT + 1 if j == 1 else 2 * FINISH_AT
+                for c in range(FINISH_AT, finish):
                     vector_chunk(j, c)
                 if j > 0:
                     invert(j - 1)
                     if j <= 2:
                         normalise_early(j - 1)
-                for c in range(2 * FINISH_AT, VECTOR_CHUNKS):
+                for c in range(finish, VECTOR_CHUNKS):
                     vector_chunk(j, c)
                 scalar_moments(j, 0, own, sums, scratch)
                 own = scalar_sum(j, 1, scratch)
                 scalar_moments(j, 1, own, sums, scratch)
-            aggregate(ROW_TILES - 1)
-            root(ROW_TILES - 1)
-
             ln_t = psum_t.tile([P, PACK, P], BF16, tag="xt")
             for t in range(PACK):
                 nc.tensor.transpose(ln_t[:, t, :], ln_rows[:, t:K_PASS:PACK], ident_bf16[:])
             ln_cols = const.tile([P, PACK, 2 * GROUPS], F32)
             nc.vector.tensor_copy(out=ln_cols[:], in_=ln_t[:, :, 0 : 2 * GROUPS])
+            for g in range(2):
+                for j in range(1, ROW_TILES - 1):
+                    normalise_one(j, g)
+            keep_busy(8, ROWS)
+            turn(0, range(ROW_TILES - 1))
+            aggregate(ROW_TILES - 1)
+            root(ROW_TILES - 1)
             invert(ROW_TILES - 1)
 
-        work = ctx.enter_context(tc.tile_pool(name="work", bufs=6))
         stage = ctx.enter_context(tc.tile_pool(name="stage", bufs=2))
 
-        acc = [psum_acc.tile([P, ROWS], F32, name="acc%d" % w) for w in range(3)]
+        acc = [psum_acc.tile([P, ROWS], F32, name="acc%d" % w, tag="acc%d" % w) for w in range(3)]
         planes = {}
         grouped = {}
         codes = {}
         code_scales = {}
+        turned = {}
 
         def normalise_rest(g):
             for j in range(ROW_TILES):
                 if (j, g) not in unit:
-                    made = work.tile([P, PACK, P], F32, name="made", tag="work")
-                    unit[j, g] = made[:]
-                    nc.vector.tensor_scalar(
-                        out=unit[j, g],
-                        in0=unit_columns(j, g),
-                        scalar1=mean[j],
-                        scalar2=rstd[j],
-                        op0=ALU.subtract,
-                        op1=ALU.mult,
-                    )
+                    normalise_one(j, g)
 
-        def turn_and_scale(g):
-            planes[g] = stage.tile([P, PACK, ROWS], BF16, name="planes", tag="planes")
+        def scale(g, rows):
+            if g not in planes:
+                planes[g] = stage.tile([P, PACK, ROWS], BF16, name="planes", tag="planes")
             for t in range(PACK):
-                xt = psum_t.tile([P, ROWS], F32, tag="xt")
-                for j in range(ROW_TILES):
-                    nc.tensor.transpose(xt[:, j * P : (j + 1) * P], unit[j, g][:, t, :], ident_f32[:])
                 nc.scalar.activation(
-                    out=planes[g][:, t, :],
-                    in_=xt[:],
+                    out=planes[g][:, t, rows],
+                    in_=turned_units[g][t][:, rows],
                     func=ACT.Identity,
                     scale=ln_cols[:, t, g : g + 1],
                     bias=ln_cols[:, t, GROUPS + g : GROUPS + g + 1],
                 )
 
-        def regroup(g):
-            grouped[g] = stage.tile([P, ROWS, PACK], BF16, name="grouped", tag="grouped", align_bytes=64)
+        def regroup(g, rows):
+            if g not in grouped:
+                grouped[g] = stage.tile([P, ROWS, PACK], BF16, name="grouped", tag="grouped", align_bytes=64)
             nc.vector.tensor_copy(
-                out=grouped[g][:].rearrange("p (c i) t -> p c t i", i=RUN),
-                in_=planes[g][:].rearrange("p t (c i) -> p c t i", i=RUN),
+                out=grouped[g][:, rows, :].rearrange("p (c i) t -> p c t i", i=RUN),
+                in_=planes[g][:, :, rows].rearrange("p t (c i) -> p c t i", i=RUN),
             )
 
-        def quantise(g):
-            codes[g] = stage.tile([P, ROWS], U32, name="codes", tag="codes", align_bytes=64)
-            code_scales[g] = stage.tile([P, ROWS], U8, name="code_scales", tag="code_scales", align_bytes=64)
+        def quantise(g, rows):
+            if g not in codes:
+                codes[g] = stage.tile([P, ROWS], U32, name="codes", tag="codes", align_bytes=64)
+                code_scales[g] = stage.tile([P, ROWS], U8, name="code_scales", tag="code_scales", align_bytes=64)
             nc.vector.quantize_mx(
-                out=codes[g][:].bitcast(FP8X4),
-                scales=code_scales[g][:],
-                in_=grouped[g][:].rearrange("p r t -> p (r t)"),
+                out=codes[g][:, rows].bitcast(FP8X4),
+                scales=code_scales[g][:, rows],
+                in_=grouped[g][:, rows, :].rearrange("p r t -> p (r t)"),
             )
 
-        def project(g):
+        def project(g, rows):
             for w in range(3):
                 nc.tensor.matmul_mx(
-                    out=acc[w][:],
+                    out=acc[w][:, rows],
                     lhsT=w_words[g // WORD_GROUPS][:, w, g % WORD_GROUPS, :].bitcast(FP8X4),
                     lhsT_scale=w_planes[:, w, g, :],
-                    rhs=codes[g][:].bitcast(FP8X4),
-                    rhs_scale=code_scales[g][:],
+                    rhs=codes[g][:, rows].bitcast(FP8X4),
+                    rhs_scale=code_scales[g][:, rows],
                     start=(g == 0),
-                    stop=(g == GROUPS - 1),
+                    stop=(g == GROUPS - 1 and rows.stop == ROWS),
                 )
 
+        def stay_busy(g):
+            unread = psum_t.tile([P, ROWS], F32, name="unread_product", tag="xt")
+            nc.tensor.matmul_mx(
+                out=unread[:, halves[0]],
+                lhsT=w_words[g // WORD_GROUPS][:, 0, g % WORD_GROUPS, :].bitcast(FP8X4),
+                lhsT_scale=w_planes[:, 0, g, :],
+                rhs=codes[g][:, halves[0]].bitcast(FP8X4),
+                rhs_scale=code_scales[g][:, halves[0]],
+                start=True,
+                stop=True,
+            )
+
+        last = GROUPS - 1
+        every = slice(0, ROWS)
+        halves = [slice(0, ROWS // 2), slice(ROWS // 2, ROWS)]
         with tc.manual_schedule():
-            for step in range(GROUPS + 4):
+            for step in range(GROUPS + 2):
                 if step < GROUPS:
                     normalise_rest(step)
                 if 0 <= step - 1 < GROUPS:
-                    turn_and_scale(step - 1)
-                if 0 <= step - 2 < GROUPS:
-                    regroup(step - 2)
-                if 0 <= step - 3 < GROUPS:
-                    quantise(step - 3)
-                if 0 <= step - 4 < GROUPS:
-                    project(step - 4)
+                    turn(step - 1, range(ROW_TILES - 1, ROW_TILES) if step == 1 else range(ROW_TILES))
+                if 0 <= step - 1 < last:
+                    scale(step - 1, every)
+                if step - 1 == last:
+                    for rows in halves:
+                        scale(last, rows)
+                if 0 <= step - 2 < last:
+                    regroup(step - 2, every)
+                if 0 <= step - 3 < last:
+                    quantise(step - 3, every)
+                if 1 <= step < 4:
+                    keep_busy(3, ROWS)
+                if 0 <= step - 4 < last:
+                    project(step - 4, every)
+                    stay_busy(step - 4)
                     if (step - 3) % WORD_GROUPS == 0 and len(w_words) * WORD_GROUPS < GROUPS:
                         load_words()
+            for rows in halves:
+                regroup(last, rows)
+            for rows in halves:
+                quantise(last, rows)
+            project(last - 1, every)
+            for rows in halves:
+                project(last, rows)
 
-        by_feature = []
-        for w in range(3):
-            by_feature_w = work.tile([P, ROWS], F32, name="by_feature_w", tag="work")
-            if w == 1:
-                nc.scalar.copy(out=by_feature_w[:], in_=acc[w][:])
-            else:
-                nc.vector.tensor_copy(out=by_feature_w[:], in_=acc[w][:])
-            by_feature.append(by_feature_w)
-        for j in range(ROW_TILES):
-            turned = psum_t.tile([P, 3, E], F32, tag="xt")
-            for w in range(3):
-                nc.tensor.transpose(turned[:, w, :], by_feature[w][:, j * P : (j + 1) * P], ident_f32[:])
-            by_row = work.tile([P, 3, E], F32, name="by_row", tag="work")
-            if j % 2 == 0:
-                nc.vector.tensor_copy(out=by_row[:], in_=turned[:])
-            else:
-                nc.scalar.copy(out=by_row[:], in_=turned[:])
-            for w in range(3):
-                nc.sync.dma_start(out=outs[w][j * P : (j + 1) * P, :], in_=by_row[:, w, :])
+            by_feature = [work.tile([P, ROWS], F32, name="by_feature%d" % w, tag="work") for w in range(3)]
+            for rows in halves:
+                middle = slice(rows.start, rows.start + P)
+                rest = slice(rows.start + P, rows.stop)
+                nc.vector.tensor_copy(out=by_feature[0][:, rows], in_=acc[0][:, rows])
+                nc.scalar.copy(out=by_feature[1][:, rows], in_=acc[1][:, rows])
+                nc.vector.tensor_copy(out=by_feature[2][:, middle], in_=acc[2][:, middle])
+                nc.scalar.copy(out=by_feature[2][:, rest], in_=acc[2][:, rest])
+                for j in range(rows.start // P, rows.stop // P):
+                    turned[j] = psum_t.tile([P, 3, E], F32, name="turned_j", tag="xt")
+                    for w in range(3):
+                        nc.tensor.transpose(turned[j][:, w, :], by_feature[w][:, j * P : (j + 1) * P], ident_f32[:])
+            for j in range(ROW_TILES):
+                by_row = work.tile([P, 3, E], F32, name="by_row", tag="work")
+                if j % 2 == 0:
+                    nc.vector.tensor_copy(out=by_row[:], in_=turned[j][:])
+                else:
+                    nc.scalar.copy(out=by_row[:], in_=turned[j][:])
+                for w in range(3):
+                    nc.sync.dma_start(out=outs[w][j * P : (j + 1) * P, :], in_=by_row[:, w, :])

from contextlib import ExitStack

import concourse.mybir as mybir
from concourse.masks import make_identity

F32 = mybir.dt.float32
BF16 = mybir.dt.bfloat16
I32 = mybir.dt.int32
U32 = mybir.dt.uint32
U8 = mybir.dt.uint8
FP8X4 = mybir.dt.float8_e4m3fn_x4
ALU = mybir.AluOpType
ACT = mybir.ActivationFunctionType

P = 128
PACK = 4
K_PASS = P * PACK
ROWS = 512
D = 16384
E = 128
ROW_TILES = ROWS // P
GROUPS = D // K_PASS
EPS = 1e-5
LOAD_COLS = 4096
WORD_GROUPS = 4
RUN = 4
BN_COLS = 512
SCALAR_COLS = 3328
SUM_BLOCKS = 19
SUM_COLS = SUM_BLOCKS * P
VECTOR_CHUNKS = (D - 2 * SCALAR_COLS) // BN_COLS
SLOT = 8
FINISH_AT = 4
EARLY_COLS = 1024
SPARE = 22
UNITS = 2 * SPARE - 1

FLOPS = 2 * ROWS * D * 3 * E


def tile_toyattnsublayer_pa_k_kernel(
    tc, h, ln_w, ln_b, w_q_words, w_q_scales, w_k_words, w_k_scales, w_v_words, w_v_scales, out_0, out_1, out_2
):
    nc = tc.nc
    words_in = [w_q_words, w_k_words, w_v_words]
    scales_in = [w_q_scales, w_k_scales, w_v_scales]
    outs = [out_0, out_1, out_2]

    with ExitStack() as ctx:
        const = ctx.enter_context(tc.tile_pool(name="const", bufs=1))
        small = ctx.enter_context(tc.tile_pool(name="small", bufs=1))
        psum_acc = ctx.enter_context(tc.psum_pool(name="psum_acc", bufs=1))
        psum_t = ctx.enter_context(tc.psum_pool(name="psum_t", bufs=5))

        warm = small.tile([P, 1], F32)
        nc.gpsimd.memset(warm[:], 1.0)
        nc.scalar.sqrt(out=warm[:], in_=warm[:])
        ident_bf16 = const.tile([P, P], BF16)
        make_identity(nc, ident_bf16[:])
        stats = []
        for j in range(ROW_TILES):
            stats_j = small.tile([P, VECTOR_CHUNKS + 1, SLOT], F32, name="stats%d" % j)
            nc.gpsimd.memset(stats_j[:, VECTOR_CHUNKS, 0:6], float(SCALAR_COLS))
            stats.append(stats_j)
        ident_f32 = const.tile([P, P], F32)
        make_identity(nc, ident_f32[:])
        w_planes = const.tile([P, 3, GROUPS, E], U8, align_bytes=64)
        nc.gpsimd.memset(w_planes[:].bitcast(I32), 0)
        ln_rows = const.tile([P, K_PASS], BF16)
        nc.gpsimd.memset(ln_rows[:], 0.0)
        spare = const.tile([P, SPARE, PACK, P], F32)

        h_sb = [const.tile([P, D], BF16, name="h_sb%d" % j) for j in range(ROW_TILES)]

        def load_h(j, first, last):
            nc.sync.dma_start(out=h_sb[j][:, first:last], in_=h[j * P : (j + 1) * P, first:last])

        load_h(0, SCALAR_COLS, SCALAR_COLS + EARLY_COLS)
        load_h(0, SUM_COLS, SCALAR_COLS)
        load_h(0, SCALAR_COLS + EARLY_COLS, SCALAR_COLS + 3 * EARLY_COLS)
        load_h(0, 0, SUM_COLS)
        load_h(0, SCALAR_COLS + 3 * EARLY_COLS, SCALAR_COLS + 5 * EARLY_COLS)
        load_h(0, SCALAR_COLS + 5 * EARLY_COLS, D - SCALAR_COLS)
        load_h(0, D - SCALAR_COLS, D)
        for j in range(1, ROW_TILES):
            for c in range(0, D, LOAD_COLS):
                load_h(j, c, c + LOAD_COLS)
        nc.sync.dma_start(out=ln_rows[0:GROUPS, :], in_=ln_w.rearrange("(g c) -> g c", c=K_PASS))
        nc.sync.dma_start(out=ln_rows[GROUPS : 2 * GROUPS, :], in_=ln_b.rearrange("(g c) -> g c", c=K_PASS))
        for w in range(3):
            for quad in range(4):
                nc.sync.dma_start(
                    out=w_planes[32 * quad : 32 * quad + 4, w, :, :].bitcast(I32),
                    in_=scales_in[w][:, 4 * quad : 4 * quad + 4, :].rearrange("g q n -> q g n").bitcast(I32),
                )
        words_pool = ctx.enter_context(tc.tile_pool(name="words", bufs=2))
        w_words = []

        def load_words():
            g0 = len(w_words) * WORD_GROUPS
            chunk = words_pool.tile([P, 3, WORD_GROUPS, E], U32, name="chunk", tag="chunk", align_bytes=64)
            w_words.append(chunk)
            for w in range(3):
                nc.sync.dma_start(
                    out=chunk[:, w, :, :].bitcast(I32),
                    in_=words_in[w].rearrange("g p n t -> p g (n t)")[:, g0 : g0 + WORD_GROUPS, :].bitcast(I32),
                )

        load_words()
        load_words()

        mean = {}
        rstd = {}
        var_eps = {}

        def column(name):
            return small.tile([P, 1], F32, name=name)

        def vector_chunk(j, c):
            first = SCALAR_COLS + c * BN_COLS
            nc.vector.bn_stats(out=stats[j][:, c, 0:6], in_=h_sb[j][:, first : first + BN_COLS])

        def sum_blocks(j):
            sums = [psum_acc.tile([P, P], F32, name="sums%d" % a, tag="acc%d" % ((2 * j + a) % 3)) for a in range(2)]
            for a in range(2):
                first = a * (D - SCALAR_COLS)
                for b in range(SUM_BLOCKS):
                    nc.tensor.matmul(
                        out=sums[a][:],
                        lhsT=ident_bf16[:],
                        rhs=h_sb[j][:, first + b * P : first + (b + 1) * P],
                        start=(b == 0),
                        stop=(b == SUM_BLOCKS - 1),
                    )
            return sums

        def scalar_sum(j, a, scratch):
            first = a * (D - SCALAR_COLS)
            own = column("own%d_%d" % (j, a))
            unread = scratch.tile([P, SCALAR_COLS], BF16, name="unread", tag="unread")
            nc.scalar.activation(
                out=unread[:, 0 : SCALAR_COLS - SUM_COLS],
                in_=h_sb[j][:, first + SUM_COLS : first + SCALAR_COLS],
                func=ACT.Identity,
                scale=1.0 / (SCALAR_COLS * P),
                accum_out=own[:],
            )
            return own

        def scalar_moments(j, a, own, sums, scratch):
            first = a * (D - SCALAR_COLS)
            shift = stats[j][:, 0, 1:2]
            mean_at, m2_at = [stats[j][:, VECTOR_CHUNKS, 3 * a + i : 3 * a + i + 1] for i in (1, 2)]
            squares = column("squares%d_%d" % (j, a))
            unread = scratch.tile([P, SCALAR_COLS], BF16, name="unread", tag="unread")
            nc.scalar.activation(
                out=unread[:],
                in_=h_sb[j][:, first : first + SCALAR_COLS],
                func=ACT.Square,
                scale=-1.0,
                bias=shift,
                accum_out=squares[:],
            )
            unread = scratch.tile([P, SCALAR_COLS], BF16, name="unread", tag="unread")
            nc.scalar.activation(
                out=unread[:, 0:P],
                in_=sums[a][:],
                func=ACT.Identity,
                scale=1.0 / SCALAR_COLS,
                bias=own[:],
                accum_out=mean_at,
            )
            offset = column("offset%d_%d" % (j, a))
            nc.scalar.activation(out=offset[:], in_=mean_at, func=ACT.Square, scale=-1.0, bias=shift)
            nc.scalar.activation(out=m2_at, in_=offset[:], func=ACT.Identity, scale=-float(SCALAR_COLS), bias=squares[:])

        def aggregate(j):
            mean_var = small.tile([P, 2], F32, name="mean_var%d" % j)
            nc.vector.bn_aggr(out=mean_var[:], in_=stats[j][:, :, 0:6])
            var_eps[j] = column("var_eps%d" % j)
            nc.vector.tensor_scalar_add(out=var_eps[j][:], in0=mean_var[:, 1:2], scalar1=EPS)
            mean[j] = mean_var[:, 0:1]

        def root(j):
            nc.scalar.sqrt(out=var_eps[j][:], in_=var_eps[j][:])

        def invert(j):
            rstd_j = column("rstd%d" % j)
            nc.vector.reciprocal(out=rstd_j[:], in_=var_eps[j][:])
            rstd[j] = rstd_j[:, 0:1]

        early = [(0, g) for g in range(GROUPS)] + [(1, g) for g in range(2 * GROUPS - UNITS, GROUPS)]
        unit = {}

        def unit_columns(j, g):
            return h_sb[j][:, g * K_PASS : (g + 1) * K_PASS].rearrange("r (p t) -> r t p", t=PACK)

        def normalise_early(j):
            minus = column("minus%d" % j)
            nc.gpsimd.tensor_scalar(
                out=minus[:], in0=mean[j], scalar1=rstd[j], scalar2=-1.0, op0=ALU.mult, op1=ALU.mult
            )
            for n, (row_tile, g) in enumerate(early):
                if row_tile == j:
                    if n < SPARE:
                        unit[j, g] = spare[:, n, :, :]
                    else:
                        used_j, used_g = early[2 * (n - SPARE)]
                        used = h_sb[used_j][:, used_g * K_PASS : (used_g + 2) * K_PASS].bitcast(F32)
                        unit[j, g] = used.rearrange("r (t p) -> r t p", t=PACK)
                    nc.gpsimd.tensor_scalar(
                        out=unit[j, g],
                        in0=unit_columns(j, g),
                        scalar1=rstd[j],
                        scalar2=minus[:],
                        op0=ALU.mult,
                        op1=ALU.add,
                    )

        work = ctx.enter_context(tc.tile_pool(name="work", bufs=6))

        def normalise_one(j, g):
            made = work.tile([P, PACK, P], F32, name="made", tag="work")
            unit[j, g] = made[:]
            nc.vector.tensor_scalar(
                out=unit[j, g],
                in0=unit_columns(j, g),
                scalar1=mean[j],
                scalar2=rstd[j],
                op0=ALU.subtract,
                op1=ALU.mult,
            )

        turned_units = {}

        def turn(g, tiles):
            if g not in turned_units:
                turned_units[g] = [psum_t.tile([P, ROWS], F32, name="xt%d" % t, tag="xt") for t in range(PACK)]
            for t in range(PACK):
                for j in tiles:
                    nc.tensor.transpose(
                        turned_units[g][t][:, j * P : (j + 1) * P], unit[j, g][:, t, :], ident_f32[:]
                    )

        def keep_busy(passes, columns):
            unread = psum_t.tile([P, ROWS], F32, name="unread_product", tag="xt")
            for i in range(passes):
                nc.tensor.matmul_mx(
                    out=unread[:, 0:columns],
                    lhsT=w_words[0][:, 0, 0, :].bitcast(FP8X4),
                    lhsT_scale=w_planes[:, 0, 0, :],
                    rhs=w_words[0][:, 0, :, :].rearrange("p g n -> p (g n)")[:, 0:columns].bitcast(FP8X4),
                    rhs_scale=w_planes[:, 0, 0:WORD_GROUPS, :].rearrange("p g n -> p (g n)")[:, 0:columns],
                    start=True,
                    stop=True,
                )

        with tc.manual_schedule(), tc.tile_pool(name="scratch", bufs=2) as scratch:
            for j in range(ROW_TILES):
                sums = sum_blocks(j)
                for c in range(FINISH_AT):
                    vector_chunk(j, c)
                if j > 0:
                    aggregate(j - 1)
                if j == 1:
                    root(j - 1)
                own = scalar_sum(j, 0, scratch)
                if j > 1:
                    root(j - 1)
                finish = FINISH_AT + 1 if j == 1 else 2 * FINISH_AT
                for c in range(FINISH_AT, finish):
                    vector_chunk(j, c)
                if j > 0:
                    invert(j - 1)
                    if j <= 2:
                        normalise_early(j - 1)
                for c in range(finish, VECTOR_CHUNKS):
                    vector_chunk(j, c)
                scalar_moments(j, 0, own, sums, scratch)
                own = scalar_sum(j, 1, scratch)
                scalar_moments(j, 1, own, sums, scratch)
            ln_t = psum_t.tile([P, PACK, P], BF16, tag="xt")
            for t in range(PACK):
                nc.tensor.transpose(ln_t[:, t, :], ln_rows[:, t:K_PASS:PACK], ident_bf16[:])
            ln_cols = const.tile([P, PACK, 2 * GROUPS], F32)
            nc.vector.tensor_copy(out=ln_cols[:], in_=ln_t[:, :, 0 : 2 * GROUPS])
            for g in range(2):
                for j in range(1, ROW_TILES - 1):
                    normalise_one(j, g)
            keep_busy(8, ROWS)
            turn(0, range(ROW_TILES - 1))
            aggregate(ROW_TILES - 1)
            root(ROW_TILES - 1)
            invert(ROW_TILES - 1)

        stage = ctx.enter_context(tc.tile_pool(name="stage", bufs=2))

        acc = [psum_acc.tile([P, ROWS], F32, name="acc%d" % w, tag="acc%d" % w) for w in range(3)]
        planes = {}
        grouped = {}
        codes = {}
        code_scales = {}
        turned = {}

        def normalise_rest(g):
            for j in range(ROW_TILES):
                if (j, g) not in unit:
                    normalise_one(j, g)

        def scale(g, rows):
            if g not in planes:
                planes[g] = stage.tile([P, PACK, ROWS], BF16, name="planes", tag="planes")
            for t in range(PACK):
                nc.scalar.activation(
                    out=planes[g][:, t, rows],
                    in_=turned_units[g][t][:, rows],
                    func=ACT.Identity,
                    scale=ln_cols[:, t, g : g + 1],
                    bias=ln_cols[:, t, GROUPS + g : GROUPS + g + 1],
                )

        def regroup(g, rows):
            if g not in grouped:
                grouped[g] = stage.tile([P, ROWS, PACK], BF16, name="grouped", tag="grouped", align_bytes=64)
            nc.vector.tensor_copy(
                out=grouped[g][:, rows, :].rearrange("p (c i) t -> p c t i", i=RUN),
                in_=planes[g][:, :, rows].rearrange("p t (c i) -> p c t i", i=RUN),
            )

        def quantise(g, rows):
            if g not in codes:
                codes[g] = stage.tile([P, ROWS], U32, name="codes", tag="codes", align_bytes=64)
                code_scales[g] = stage.tile([P, ROWS], U8, name="code_scales", tag="code_scales", align_bytes=64)
            nc.vector.quantize_mx(
                out=codes[g][:, rows].bitcast(FP8X4),
                scales=code_scales[g][:, rows],
                in_=grouped[g][:, rows, :].rearrange("p r t -> p (r t)"),
            )

        def project(g, rows):
            for w in range(3):
                nc.tensor.matmul_mx(
                    out=acc[w][:, rows],
                    lhsT=w_words[g // WORD_GROUPS][:, w, g % WORD_GROUPS, :].bitcast(FP8X4),
                    lhsT_scale=w_planes[:, w, g, :],
                    rhs=codes[g][:, rows].bitcast(FP8X4),
                    rhs_scale=code_scales[g][:, rows],
                    start=(g == 0),
                    stop=(g == GROUPS - 1 and rows.stop == ROWS),
                )

        def stay_busy(g):
            unread = psum_t.tile([P, ROWS], F32, name="unread_product", tag="xt")
            nc.tensor.matmul_mx(
                out=unread[:, halves[0]],
                lhsT=w_words[g // WORD_GROUPS][:, 0, g % WORD_GROUPS, :].bitcast(FP8X4),
                lhsT_scale=w_planes[:, 0, g, :],
                rhs=codes[g][:, halves[0]].bitcast(FP8X4),
                rhs_scale=code_scales[g][:, halves[0]],
                start=True,
                stop=True,
            )

        last = GROUPS - 1
        every = slice(0, ROWS)
        halves = [slice(0, ROWS // 2), slice(ROWS // 2, ROWS)]
        with tc.manual_schedule():
            for step in range(GROUPS + 2):
                if step < GROUPS:
                    normalise_rest(step)
                if 0 <= step - 1 < GROUPS:
                    turn(step - 1, range(ROW_TILES - 1, ROW_TILES) if step == 1 else range(ROW_TILES))
                if 0 <= step - 1 < last:
                    scale(step - 1, every)
                if step - 1 == last:
                    for rows in halves:
                        scale(last, rows)
                if 0 <= step - 2 < last:
                    regroup(step - 2, every)
                if 0 <= step - 3 < last:
                    quantise(step - 3, every)
                if 1 <= step < 4:
                    keep_busy(3, ROWS)
                if 0 <= step - 4 < last:
                    project(step - 4, every)
                    stay_busy(step - 4)
                    if (step - 3) % WORD_GROUPS == 0 and len(w_words) * WORD_GROUPS < GROUPS:
                        load_words()
            for rows in halves:
                regroup(last, rows)
            for rows in halves:
                quantise(last, rows)
            project(last - 1, every)
            for rows in halves:
                project(last, rows)

            by_feature = [work.tile([P, ROWS], F32, name="by_feature%d" % w, tag="work") for w in range(3)]
            for rows in halves:
                middle = slice(rows.start, rows.start + P)
                rest = slice(rows.start + P, rows.stop)
                nc.vector.tensor_copy(out=by_feature[0][:, rows], in_=acc[0][:, rows])
                nc.scalar.copy(out=by_feature[1][:, rows], in_=acc[1][:, rows])
                nc.vector.tensor_copy(out=by_feature[2][:, middle], in_=acc[2][:, middle])
                nc.scalar.copy(out=by_feature[2][:, rest], in_=acc[2][:, rest])
                for j in range(rows.start // P, rows.stop // P):
                    turned[j] = psum_t.tile([P, 3, E], F32, name="turned_j", tag="xt")
                    for w in range(3):
                        nc.tensor.transpose(turned[j][:, w, :], by_feature[w][:, j * P : (j + 1) * P], ident_f32[:])
            for j in range(ROW_TILES):
                by_row = work.tile([P, 3, E], F32, name="by_row", tag="work")
                if j % 2 == 0:
                    nc.vector.tensor_copy(out=by_row[:], in_=turned[j][:])
                else:
                    nc.scalar.copy(out=by_row[:], in_=turned[j][:])
                for w in range(3):
                    nc.sync.dma_start(out=outs[w][j * P : (j + 1) * P, :], in_=by_row[:, w, :])
